import numpy as np
import ml_dtypes


def mxq(x, axis, fmt="e4m3"):
    dtype, down = {"e4m3": (ml_dtypes.float8_e4m3fn, 7), "e5m2": (ml_dtypes.float8_e5m2, 14)}[fmt]
    v = np.moveaxis(np.asarray(x, np.float32).astype(ml_dtypes.bfloat16).astype(np.float64), axis, -1)
    blocks = v.reshape(v.shape[:-1] + (-1, 32))
    amax = np.abs(blocks).max(-1, keepdims=True)
    byte = np.maximum(np.where(amax > 0, np.frexp(amax)[1] - 1 + 127, 0) - down, 1)
    scale = np.exp2(byte - 127.0)
    codes = (blocks / scale).astype(np.float32).astype(dtype).astype(np.float64)
    return np.moveaxis((codes * scale).reshape(v.shape), -1, axis)


WIDE = False


def mx_kscale(k):
    if not WIDE:
        return np.ones(k)
    levels = np.array([30, -30])
    if k % 512:
        return np.exp2(np.random.permutation(np.resize(levels, k // 32))).repeat(32)
    a = np.empty((k // 512, 16))
    for p in range(k // 512):
        a[p, :8] = np.random.permutation(np.resize(levels, 8))
        for g in range(8):
            far = levels[np.abs(levels - a[p, g]) >= 10]
            a[p, g + 8] = far[np.random.randint(len(far))]
    return np.exp2(a.ravel()).repeat(32)


BF16 = ml_dtypes.bfloat16


def bf(x):
    return np.asarray(x, np.float32).astype(BF16)


def f64(x):
    return np.asarray(x).astype(np.float64)


E2M1 = np.array([0.0, 0.5, 1.0, 1.5, 2.0, 3.0, 4.0, 6.0, -0.0, -0.5, -1.0, -1.5, -2.0, -3.0, -4.0, -6.0])


def pack_weight(w, fmt):
    k, n = w.shape
    w = f64(bf(w)).reshape(k // 32, 32, n)
    amax = np.abs(w).max(1)
    if fmt == "e4m3":
        byte = np.frexp(amax)[1] - 1 + 127 - 7
    else:
        mant, ex = np.frexp(amax / 6.0)
        byte = np.where(mant > 0.5, ex, ex - 1) + 127
    byte = np.clip(np.where(amax > 0, byte, 1), 1, 254)
    scaled = (w * np.exp2(127.0 - byte)[:, None, :]).reshape(k, n).astype(np.float32)
    by_word = np.ascontiguousarray(scaled.reshape(k // 512, 128, 4, n).transpose(0, 1, 3, 2))
    if fmt == "e4m3":
        words = by_word.astype(ml_dtypes.float8_e4m3fn).view(np.uint8)
    else:
        c = by_word.astype(ml_dtypes.float4_e2m1fn).view(np.uint8) & 0xF
        words = c[..., 0::2] | (c[..., 1::2] << 4)
    return np.ascontiguousarray(words), np.ascontiguousarray(byte.astype(np.uint8).reshape(k // 512, 16, n))


def unpack_weight(words, scales, fmt):
    g, p, n, _ = words.shape
    if fmt == "e4m3":
        vals = np.ascontiguousarray(words).view(ml_dtypes.float8_e4m3fn).astype(np.float64)
    else:
        nib = np.empty((g, p, n, 4), np.uint8)
        nib[..., 0::2] = words & 0xF
        nib[..., 1::2] = words >> 4
        vals = E2M1[nib]
    vals = vals * np.repeat(np.exp2(scales.astype(np.float64) - 127.0), 8, axis=1)[..., None]
    return vals.transpose(0, 1, 3, 2).reshape(g * 512, n)

def pack4(w):
    words, scales = pack_weight(w, "e2m1")
    return words.reshape(words.shape[0], 128, -1), scales


def unpack4(words, scales):
    return unpack_weight(words.reshape(words.shape[0], 128, -1, 2), scales, "e2m1")


B, L, C, H, DH, AX = 2, 1024, 1536, 16, 96, 3
D3 = DH // AX
HALF = D3 // 2
ROPE_BASE = 10000.0
COORD_MAX = 10.0


def rope_3d(x, coords):
    inv_freq = 1.0 / (ROPE_BASE ** (np.arange(HALF) / HALF))
    ang = coords[..., None] * inv_freq
    cos = np.cos(ang)[:, None]
    sin = np.sin(ang)[:, None]
    xr = x.reshape(B, H, L, AX, D3)
    x1, x2 = xr[..., :HALF], xr[..., HALF:]
    out = np.concatenate([x1 * cos - x2 * sin, x1 * sin + x2 * cos], axis=-1)
    return out.reshape(B, H, L, DH)


def setup_inputs():
    s = mx_kscale(C)
    x_in = bf(np.random.standard_normal((B, L, C)) * s)
    coords = bf(np.random.uniform(size=(B, L, AX)) * COORD_MAX)
    w = np.random.standard_normal((H * DH, C)) * 1.5 / np.sqrt(C) / s
    words, scales = pack4(np.ascontiguousarray(w.T))
    return {"x_in": x_in,
            "coords": coords,
            "w_words": words,
            "w_scales": scales}


def reference(x_in, coords, w_words, w_scales):
    p = mxq(f64(x_in), 2, "e5m2") @ unpack4(w_words, w_scales)
    p = p.reshape(B, L, H, DH).transpose(0, 2, 1, 3)
    return rope_3d(p, f64(coords))

@@ -1,0 +1,260 @@
+import math
+from contextlib import ExitStack
+
+import concourse.mybir as mybir
+from concourse.masks import make_identity
+
+B, L, C, H, DH, AX = 2, 1024, 1536, 16, 96, 3
+HALF = 16
+BLK = 2 * HALF
+ROPE_BASE = 10000.0
+FLOPS = 2 * B * L * C * H * DH
+
+F32 = mybir.dt.float32
+BF16 = mybir.dt.bfloat16
+I32 = mybir.dt.int32
+U32 = mybir.dt.uint32
+U8 = mybir.dt.uint8
+E5M2X4 = mybir.dt.float8_e5m2_x4
+E2M1X4 = mybir.dt.float4_e2m1fn_x4
+ALU = mybir.AluOpType
+ACT = mybir.ActivationFunctionType
+
+P = 128
+PASSES = C // 512
+TILES_PER_BATCH = L // P
+PAIRS = B * TILES_PER_BATCH // 2
+HEADS_PER_BANK = 4
+BANK_COLS = HEADS_PER_BANK * DH
+BANKS_PER_TILE = H // HEADS_PER_BANK
+GROUPS = ((0, 256), (256, 128))
+SIN, COS, NEG_SIN = 0, 1, 2
+
+
+def tile_crossattnrope_pa_kernel(tc, x_in, coords, w_words, w_scales, out):
+    nc = tc.nc
+    x_rows = [x_in[b].rearrange("(p j) k -> p j k", j=TILES_PER_BATCH) for b in range(B)]
+    out_rows = [out[b].rearrange("h (p j) d -> p h (j d)", j=TILES_PER_BATCH) for b in range(B)]
+
+    with ExitStack() as ctx:
+        keep = ctx.enter_context(tc.tile_pool(name="keep", bufs=1))
+        work = ctx.enter_context(tc.tile_pool(name="work", bufs=3))
+        turn_ps = ctx.enter_context(tc.psum_pool(name="turn_ps", bufs=3))
+        acc_ps = ctx.enter_context(tc.psum_pool(name="acc_ps", bufs=5))
+        ctx.enter_context(tc.manual_schedule())
+
+        w_scale = keep.tile([P, PASSES, C], U8, align_bytes=64)
+        nc.gpsimd.memset(w_scale[:].bitcast(I32), 0)
+        ident = keep.tile([P, P], F32)
+        make_identity(nc, ident[:])
+
+        coord_sb = keep.tile([P, B, TILES_PER_BATCH * AX], BF16)
+        nc.sync.dma_start(out=coord_sb[:], in_=coords.rearrange("b (p j) a -> p b (j a)", j=TILES_PER_BATCH))
+
+        x_sb = {}
+
+        def load_x(t0, count):
+            b, j = divmod(t0, TILES_PER_BATCH)
+            xt = keep.tile([P, count, C], BF16, name="x%d" % t0, align_bytes=64)
+            nc.sync.dma_start(out=xt[:], in_=x_rows[b][:, j : j + count, :])
+            for s in range(count):
+                x_sb[t0 + s] = xt[:, s, :]
+
+        load_x(0, 1)
+        for q in range(4):
+            nc.sync.dma_start(
+                out=w_scale[32 * q : 32 * q + 4, :, :].bitcast(I32),
+                in_=w_scales[:, 4 * q : 4 * q + 4, :].rearrange("g r n -> r g n").bitcast(I32),
+            )
+        w_codes = []
+        for g in range(PASSES):
+            wc = keep.tile([P, 2 * C], U8, name="w_codes%d" % g, align_bytes=64)
+            nc.sync.dma_start(out=wc[:].bitcast(I32), in_=w_words[g].bitcast(I32))
+            w_codes.append(wc)
+        load_x(1, 1)
+        for pair in range(1, PAIRS):
+            load_x(2 * pair, 2)
+
+        ones = keep.tile([P, 1], F32)
+        nc.vector.memset(ones[:], 1.0)
+        turns_per_unit = keep.tile([P, 1, HALF], F32)
+        for i in range(HALF):
+            nc.vector.tensor_scalar(
+                out=turns_per_unit[:, 0, i : i + 1],
+                in0=ones[:],
+                scalar1=ROPE_BASE ** (-i / HALF) / (2 * math.pi),
+                scalar2=None,
+                op0=ALU.mult,
+            )
+
+        n_t = B * TILES_PER_BATCH
+        n_ang = n_t * AX * HALF
+        frac = keep.tile([P, 2, n_t, AX * HALF], F32)
+        table = keep.tile([P, n_t, 3, AX * HALF], F32)
+
+        def reduce_angles():
+            turns = keep.tile([P, n_ang], F32)
+            nc.vector.tensor_tensor(
+                out=turns[:].rearrange("p (c i) -> p c i", i=HALF),
+                in0=coord_sb[:].rearrange("p b c -> p (b c)").unsqueeze(2).to_broadcast([P, n_t * AX, HALF]),
+                in1=turns_per_unit[:].to_broadcast([P, n_t * AX, HALF]),
+                op=ALU.mult,
+            )
+            whole = keep.tile([P, 2, n_ang], I32)
+            nc.vector.tensor_scalar(out=whole[:, COS, :], in0=turns[:], scalar1=0.25, scalar2=None, op0=ALU.add)
+            nc.vector.tensor_copy(out=whole[:, SIN, :], in_=turns[:])
+            nc.vector.scalar_tensor_tensor(
+                out=frac[:, COS, :, :].rearrange("p t x -> p (t x)"),
+                in0=turns[:],
+                scalar=0.25,
+                in1=whole[:, COS, :],
+                op0=ALU.add,
+                op1=ALU.subtract,
+            )
+            nc.vector.tensor_tensor(
+                out=frac[:, SIN, :, :].rearrange("p t x -> p (t x)"),
+                in0=turns[:],
+                in1=whole[:, SIN, :],
+                op=ALU.subtract,
+            )
+
+        def make_tables(tiles):
+            nc.scalar.activation(
+                out=table[:, tiles, SIN : COS + 1, :].rearrange("p t s x -> p s t x"),
+                in_=frac[:, :, tiles, :],
+                func=ACT.Sin,
+                scale=2 * math.pi,
+            )
+            nc.scalar.activation(
+                out=table[:, tiles, NEG_SIN, :], in_=frac[:, SIN, tiles, :], func=ACT.Sin, scale=-2 * math.pi
+            )
+
+        staged = {}
+
+        def open_pair(pair):
+            grouped = work.tile([P, 2 * PASSES, 512], BF16, align_bytes=64)
+            codes = work.tile([P, 2 * PASSES, P], U32, align_bytes=64)
+            scales = work.tile([P, 2 * PASSES, P], U8, align_bytes=64)
+            staged[pair] = (grouped, codes, scales)
+
+        def turn(pair, first, count):
+            grouped = staged[pair][0]
+            bank = turn_ps.tile([P, 2, 2, P], F32)
+            for n in range(count):
+                s, g = divmod(first + n, PASSES)
+                words = x_sb[2 * pair + s].bitcast(F32)
+                for u in range(2):
+                    nc.tensor.transpose(bank[:, n, u, :], words[:, 256 * g + u : 256 * (g + 1) : 2], ident[:])
+            nc.scalar.copy(
+                out=grouped[:, first : first + count, :].bitcast(F32).rearrange("p n (r u) -> p n r u", u=2),
+                in_=bank[:, 0:count, :, :].rearrange("p n u r -> p n r u"),
+            )
+
+        def quantize(pair, first, count):
+            grouped, codes, scales = staged[pair]
+            units = slice(first, first + count)
+            nc.vector.quantize_mx(
+                out=codes[:, units, :].rearrange("p n r -> p (n r)").bitcast(E5M2X4),
+                scales=scales[:, units, :].rearrange("p n r -> p (n r)"),
+                in_=grouped[:, units, :].rearrange("p n c -> p (n c)"),
+            )
+
+        def mx_pass(acc, t, q, group, g):
+            pair, s = divmod(t, 2)
+            codes, scales = staged[pair][1:]
+            first, width = group
+            col = BANK_COLS * q + first
+            nc.tensor.matmul_mx(
+                out=acc[:, first : first + width],
+                lhsT=codes[:, PASSES * s + g, :].bitcast(E5M2X4),
+                lhsT_scale=scales[:, PASSES * s + g, :],
+                rhs=w_codes[g][:, 2 * col : 2 * (col + width)].bitcast(E2M1X4),
+                rhs_scale=w_scale[:, g, col : col + width],
+                start=(g == 0),
+                stop=(g == PASSES - 1),
+            )
+
+        def project(t, pass_major=False):
+            accs = [acc_ps.tile([P, BANK_COLS], F32, name="acc") for q in range(BANKS_PER_TILE)]
+            banks, passes = range(BANKS_PER_TILE), range(PASSES)
+            order = [(q, group, g) for q in banks for group in GROUPS for g in passes]
+            if pass_major:
+                order = [(q, GROUPS[0], g) for g in passes[:-1] for q in banks]
+                for q in banks:
+                    order += [(q, GROUPS[0], passes[-1])] + [(q, GROUPS[1], g) for g in passes]
+            for q, group, g in order:
+                mx_pass(accs[q], t, q, group, g)
+            return accs
+
+        def multiply(terms, acc, t, q):
+            x12 = acc[:].rearrange("p (h a f i) -> p f h a i", a=AX, f=2, i=HALF)
+            heads = slice(HEADS_PER_BANK * q, HEADS_PER_BANK * (q + 1))
+            for half, first in ((0, COS), (1, SIN)):
+                factors = table[:, t, first : first + 2, :].rearrange("p s (o a i) -> p s o a i", o=1, i=HALF)
+                nc.vector.tensor_tensor(
+                    out=terms[:, :, heads, :, half, :],
+                    in0=x12,
+                    in1=factors.to_broadcast([P, 2, HEADS_PER_BANK, AX, HALF]),
+                    op=ALU.mult,
+                )
+
+        def add_terms(engine, rotated, terms, heads):
+            flat = terms[:].rearrange("p c h a f i -> p c h (a f i)")
+            engine.tensor_tensor(out=rotated, in0=flat[:, 0, heads, :], in1=flat[:, 1, heads, :], op=ALU.add)
+
+        def store(rotated, t, count, heads):
+            b, j = divmod(t, TILES_PER_BATCH)
+            nc.sync.dma_start(out=out_rows[b][:, heads, DH * j : DH * (j + count)], in_=rotated)
+
+        all_heads = slice(0, H)
+
+        reduce_angles()
+        open_pair(0)
+        turn(0, 0, 2)
+        turn(0, 2, 1)
+        quantize(0, 0, 2)
+        quantize(0, 2, 1)
+        make_tables(slice(0, 2))
+
+        def turn_pair(pair):
+            open_pair(pair)
+            for n in range(PASSES):
+                turn(pair, 2 * n, 2)
+
+        for pair in range(PAIRS):
+            first, last = pair == 0, pair == PAIRS - 1
+            ta, tb = 2 * pair, 2 * pair + 1
+            if not first and not last:
+                turn_pair(pair + 1)
+            accs = project(ta, pass_major=first)
+            if first:
+                turn(0, 3, 2)
+                turn(0, 5, 1)
+                turn_pair(1)
+                make_tables(slice(2, n_t))
+            terms_a = work.tile([P, 2, H, AX, 2, HALF], F32, name="terms")
+            for q in range(BANKS_PER_TILE):
+                multiply(terms_a, accs[q], ta, q)
+                if first and q == 1:
+                    quantize(0, 3, 2)
+                    quantize(0, 5, 1)
+            if not last:
+                quantize(pair + 1, 0, 4)
+                quantize(pair + 1, 4, 2)
+            rotated = work.tile([P, H, 2 * DH], F32, name="rotated")
+            add_terms(nc.gpsimd, rotated[:, :, 0:DH], terms_a, all_heads)
+            if last:
+                store(rotated[:, :, 0:DH], ta, 1, all_heads)
+            accs = project(tb)
+            terms_b = work.tile([P, 2, H, AX, 2, HALF], F32, name="terms")
+            for q in range(BANKS_PER_TILE):
+                multiply(terms_b, accs[q], tb, q)
+            if not last:
+                add_terms(nc.gpsimd, rotated[:, :, DH : 2 * DH], terms_b, all_heads)
+                store(rotated[:], ta, 2, all_heads)
+            else:
+                for part in range(2):
+                    heads = slice(part * H // 2, (part + 1) * H // 2)
+                    final = work.tile([P, H // 2, DH], F32, name="final")
+                    add_terms(nc.vector, final[:], terms_b, heads)
+                    store(final[:], tb, 1, heads)

@@ -44,7 +44,7 @@ def tile_crossattnrope_pa_kernel(tc, x_in, coords, w_words, w_scales, out):
         ctx.enter_context(tc.manual_schedule())
 
         w_scale = keep.tile([P, PASSES, C], U8, align_bytes=64)
-        nc.gpsimd.memset(w_scale[:].bitcast(I32), 0)
+        nc.vector.memset(w_scale[:].bitcast(I32), 0)
         ident = keep.tile([P, P], F32)
         make_identity(nc, ident[:])
 
@@ -88,45 +88,41 @@ def tile_crossattnrope_pa_kernel(tc, x_in, coords, w_words, w_scales, out):
             )
 
         n_t = B * TILES_PER_BATCH
-        n_ang = n_t * AX * HALF
-        frac = keep.tile([P, 2, n_t, AX * HALF], F32)
-        table = keep.tile([P, n_t, 3, AX * HALF], F32)
+        per_tile = AX * HALF
+        coord_cols = coord_sb[:].rearrange("p b c -> p (b c)")
+        table = keep.tile([P, n_t, 3, per_tile], F32)
 
-        def reduce_angles():
-            turns = keep.tile([P, n_ang], F32)
+        def count_turns(t0, count):
+            turns = keep.tile([P, count * per_tile], F32, name="turns%d" % t0)
+            shape = [P, count * AX, HALF]
             nc.vector.tensor_tensor(
                 out=turns[:].rearrange("p (c i) -> p c i", i=HALF),
-                in0=coord_sb[:].rearrange("p b c -> p (b c)").unsqueeze(2).to_broadcast([P, n_t * AX, HALF]),
-                in1=turns_per_unit[:].to_broadcast([P, n_t * AX, HALF]),
+                in0=coord_cols[:, AX * t0 : AX * (t0 + count)].unsqueeze(2).to_broadcast(shape),
+                in1=turns_per_unit[:].to_broadcast(shape),
                 op=ALU.mult,
             )
-            whole = keep.tile([P, 2, n_ang], I32)
+            whole = keep.tile([P, 2, count * per_tile], I32, name="whole%d" % t0)
             nc.vector.tensor_scalar(out=whole[:, COS, :], in0=turns[:], scalar1=0.25, scalar2=None, op0=ALU.add)
             nc.vector.tensor_copy(out=whole[:, SIN, :], in_=turns[:])
-            nc.vector.scalar_tensor_tensor(
-                out=frac[:, COS, :, :].rearrange("p t x -> p (t x)"),
-                in0=turns[:],
-                scalar=0.25,
-                in1=whole[:, COS, :],
-                op0=ALU.add,
-                op1=ALU.subtract,
-            )
-            nc.vector.tensor_tensor(
-                out=frac[:, SIN, :, :].rearrange("p t x -> p (t x)"),
-                in0=turns[:],
-                in1=whole[:, SIN, :],
-                op=ALU.subtract,
-            )
+            return turns, whole
 
-        def make_tables(tiles):
+        def drop_whole_turns(turns, whole):
+            frac = keep.tile(whole.shape, F32, name="frac%d" % whole.shape[2])
+            nc.vector.scalar_tensor_tensor(
+                out=frac[:, COS, :], in0=turns[:], scalar=0.25, in1=whole[:, COS, :], op0=ALU.add, op1=ALU.subtract
+            )
+            nc.vector.tensor_tensor(out=frac[:, SIN, :], in0=turns[:], in1=whole[:, SIN, :], op=ALU.subtract)
+            return frac[:].rearrange("p s (t x) -> p s t x", x=per_tile)
+
+        def make_tables(tiles, frac):
             nc.scalar.activation(
                 out=table[:, tiles, SIN : COS + 1, :].rearrange("p t s x -> p s t x"),
-                in_=frac[:, :, tiles, :],
+                in_=frac,
                 func=ACT.Sin,
                 scale=2 * math.pi,
             )
             nc.scalar.activation(
-                out=table[:, tiles, NEG_SIN, :], in_=frac[:, SIN, tiles, :], func=ACT.Sin, scale=-2 * math.pi
+                out=table[:, tiles, NEG_SIN, :], in_=frac[:, SIN, :, :], func=ACT.Sin, scale=-2 * math.pi
             )
 
         staged = {}
@@ -174,16 +170,14 @@ def tile_crossattnrope_pa_kernel(tc, x_in, coords, w_words, w_scales, out):
                 stop=(g == PASSES - 1),
             )
 
-        def project(t, pass_major=False):
-            accs = [acc_ps.tile([P, BANK_COLS], F32, name="acc") for q in range(BANKS_PER_TILE)]
-            banks, passes = range(BANKS_PER_TILE), range(PASSES)
-            order = [(q, group, g) for q in banks for group in GROUPS for g in passes]
-            if pass_major:
-                order = [(q, GROUPS[0], g) for g in passes[:-1] for q in banks]
-                for q in banks:
-                    order += [(q, GROUPS[0], passes[-1])] + [(q, GROUPS[1], g) for g in passes]
-            for q, group, g in order:
-                mx_pass(accs[q], t, q, group, g)
+        def project(t):
+            accs = []
+            for q in range(BANKS_PER_TILE):
+                acc = acc_ps.tile([P, BANK_COLS], F32)
+                for group in GROUPS:
+                    for g in range(PASSES):
+                        mx_pass(acc, t, q, group, g)
+                accs.append(acc)
             return accs
 
         def multiply(terms, acc, t, q):
@@ -208,30 +202,40 @@ def tile_crossattnrope_pa_kernel(tc, x_in, coords, w_words, w_scales, out):
 
         all_heads = slice(0, H)
 
-        reduce_angles()
-        open_pair(0)
-        turn(0, 0, 2)
-        turn(0, 2, 1)
-        quantize(0, 0, 2)
-        quantize(0, 2, 1)
-        make_tables(slice(0, 2))
+        def add_and_store(engine, terms, t, parts):
+            width = H // parts
+            for part in range(parts):
+                heads = slice(part * width, (part + 1) * width)
+                piece = work.tile([P, width, DH], F32, name="piece%d" % parts, bufs=max(parts, 2))
+                add_terms(engine, piece[:], terms, heads)
+                store(piece[:], t, 1, heads)
 
         def turn_pair(pair):
             open_pair(pair)
             for n in range(PASSES):
                 turn(pair, 2 * n, 2)
 
+        make_tables(slice(0, 2), drop_whole_turns(*count_turns(0, 2)))
+        later_turns = count_turns(2, n_t - 2)
+        open_pair(0)
+        turn(0, 0, 2)
+        turn(0, 2, 1)
+        quantize(0, 0, 2)
+        quantize(0, 2, 1)
+        later_frac = drop_whole_turns(*later_turns)
+
         for pair in range(PAIRS):
             first, last = pair == 0, pair == PAIRS - 1
+            stored_together = pair < PAIRS - 2
             ta, tb = 2 * pair, 2 * pair + 1
             if not first and not last:
                 turn_pair(pair + 1)
-            accs = project(ta, pass_major=first)
+            accs = project(ta)
             if first:
                 turn(0, 3, 2)
                 turn(0, 5, 1)
                 turn_pair(1)
-                make_tables(slice(2, n_t))
+                make_tables(slice(2, n_t), later_frac)
             terms_a = work.tile([P, 2, H, AX, 2, HALF], F32, name="terms")
             for q in range(BANKS_PER_TILE):
                 multiply(terms_a, accs[q], ta, q)
@@ -240,21 +244,21 @@ def tile_crossattnrope_pa_kernel(tc, x_in, coords, w_words, w_scales, out):
                     quantize(0, 5, 1)
             if not last:
                 quantize(pair + 1, 0, 4)
-                quantize(pair + 1, 4, 2)
-            rotated = work.tile([P, H, 2 * DH], F32, name="rotated")
-            add_terms(nc.gpsimd, rotated[:, :, 0:DH], terms_a, all_heads)
-            if last:
-                store(rotated[:, :, 0:DH], ta, 1, all_heads)
+            if stored_together:
+                rotated = work.tile([P, H, 2 * DH], F32, name="rotated")
+                add_terms(nc.gpsimd, rotated[:, :, 0:DH], terms_a, all_heads)
+            else:
+                add_and_store(nc.gpsimd, terms_a, ta, 2 if last else 1)
             accs = project(tb)
             terms_b = work.tile([P, 2, H, AX, 2, HALF], F32, name="terms")
             for q in range(BANKS_PER_TILE):
                 multiply(terms_b, accs[q], tb, q)
             if not last:
+                quantize(pair + 1, 4, 2)
+            if stored_together:
                 add_terms(nc.gpsimd, rotated[:, :, DH : 2 * DH], terms_b, all_heads)
                 store(rotated[:], ta, 2, all_heads)
+            elif not last:
+                add_and_store(nc.gpsimd, terms_b, tb, 1)
             else:
-                for part in range(2):
-                    heads = slice(part * H // 2, (part + 1) * H // 2)
-                    final = work.tile([P, H // 2, DH], F32, name="final")
-                    add_terms(nc.vector, final[:], terms_b, heads)
-                    store(final[:], tb, 1, heads)
+                add_and_store(nc.vector, terms_b, tb, BANKS_PER_TILE)

@@ -27,6 +27,7 @@ PAIRS = B * TILES_PER_BATCH // 2
 HEADS_PER_BANK = 4
 BANK_COLS = HEADS_PER_BANK * DH
 BANKS_PER_TILE = H // HEADS_PER_BANK
+SHARE = 4
 GROUPS = ((0, 256), (256, 128))
 SIN, COS, NEG_SIN = 0, 1, 2
 
@@ -38,7 +39,7 @@ def tile_crossattnrope_pa_kernel(tc, x_in, coords, w_words, w_scales, out):
 
     with ExitStack() as ctx:
         keep = ctx.enter_context(tc.tile_pool(name="keep", bufs=1))
-        work = ctx.enter_context(tc.tile_pool(name="work", bufs=3))
+        work = ctx.enter_context(tc.tile_pool(name="work", bufs=2))
         turn_ps = ctx.enter_context(tc.psum_pool(name="turn_ps", bufs=3))
         acc_ps = ctx.enter_context(tc.psum_pool(name="acc_ps", bufs=5))
         ctx.enter_context(tc.manual_schedule())
@@ -60,18 +61,26 @@ def tile_crossattnrope_pa_kernel(tc, x_in, coords, w_words, w_scales, out):
             for s in range(count):
                 x_sb[t0 + s] = xt[:, s, :]
 
+        w_codes = []
+
+        def load_w(q):
+            wc = keep.tile([P, PASSES, 2 * BANK_COLS], U8, name="w_codes%d" % q, align_bytes=64)
+            cols = slice(2 * BANK_COLS * q, 2 * BANK_COLS * (q + 1))
+            nc.sync.dma_start(
+                out=wc[:].bitcast(I32), in_=w_words[:, :, cols].rearrange("g p n -> p g n").bitcast(I32)
+            )
+            w_codes.append(wc)
+
         load_x(0, 1)
+        load_x(1, 1)
+        load_w(0)
         for q in range(4):
             nc.sync.dma_start(
                 out=w_scale[32 * q : 32 * q + 4, :, :].bitcast(I32),
                 in_=w_scales[:, 4 * q : 4 * q + 4, :].rearrange("g r n -> r g n").bitcast(I32),
             )
-        w_codes = []
-        for g in range(PASSES):
-            wc = keep.tile([P, 2 * C], U8, name="w_codes%d" % g, align_bytes=64)
-            nc.sync.dma_start(out=wc[:].bitcast(I32), in_=w_words[g].bitcast(I32))
-            w_codes.append(wc)
-        load_x(1, 1)
+        for q in range(1, BANKS_PER_TILE):
+            load_w(q)
         for pair in range(1, PAIRS):
             load_x(2 * pair, 2)
 
@@ -92,7 +101,7 @@ def tile_crossattnrope_pa_kernel(tc, x_in, coords, w_words, w_scales, out):
         coord_cols = coord_sb[:].rearrange("p b c -> p (b c)")
         table = keep.tile([P, n_t, 3, per_tile], F32)
 
-        def count_turns(t0, count):
+        def reduce_angles(t0, count):
             turns = keep.tile([P, count * per_tile], F32, name="turns%d" % t0)
             shape = [P, count * AX, HALF]
             nc.vector.tensor_tensor(
@@ -101,28 +110,25 @@ def tile_crossattnrope_pa_kernel(tc, x_in, coords, w_words, w_scales, out):
                 in1=turns_per_unit[:].to_broadcast(shape),
                 op=ALU.mult,
             )
-            whole = keep.tile([P, 2, count * per_tile], I32, name="whole%d" % t0)
-            nc.vector.tensor_scalar(out=whole[:, COS, :], in0=turns[:], scalar1=0.25, scalar2=None, op0=ALU.add)
-            nc.vector.tensor_copy(out=whole[:, SIN, :], in_=turns[:])
-            return turns, whole
-
-        def drop_whole_turns(turns, whole):
-            frac = keep.tile(whole.shape, F32, name="frac%d" % whole.shape[2])
-            nc.vector.scalar_tensor_tensor(
-                out=frac[:, COS, :], in0=turns[:], scalar=0.25, in1=whole[:, COS, :], op0=ALU.add, op1=ALU.subtract
+            whole = keep.tile([P, count * per_tile], I32, name="whole%d" % t0)
+            nc.vector.tensor_copy(out=whole[:], in_=turns[:])
+            frac = keep.tile([P, count, per_tile], F32, name="frac%d" % t0)
+            nc.vector.tensor_tensor(
+                out=frac[:].rearrange("p t x -> p (t x)"), in0=turns[:], in1=whole[:], op=ALU.subtract
             )
-            nc.vector.tensor_tensor(out=frac[:, SIN, :], in0=turns[:], in1=whole[:, SIN, :], op=ALU.subtract)
-            return frac[:].rearrange("p s (t x) -> p s t x", x=per_tile)
+            return frac
 
-        def make_tables(tiles, frac):
+        def make_sin(t0, frac):
+            tiles = slice(t0, t0 + frac.shape[1])
+            nc.scalar.activation(out=table[:, tiles, SIN, :], in_=frac[:], func=ACT.Sin, scale=2 * math.pi)
+
+        def make_cos_and_neg_sin(t0, frac):
+            tiles = slice(t0, t0 + frac.shape[1])
+            size = keep.tile(frac.shape, F32, name="size%d" % t0)
+            nc.scalar.activation(out=size[:], in_=frac[:], func=ACT.Abs)
+            nc.scalar.activation(out=table[:, tiles, NEG_SIN, :], in_=frac[:], func=ACT.Sin, scale=-2 * math.pi)
             nc.scalar.activation(
-                out=table[:, tiles, SIN : COS + 1, :].rearrange("p t s x -> p s t x"),
-                in_=frac,
-                func=ACT.Sin,
-                scale=2 * math.pi,
-            )
-            nc.scalar.activation(
-                out=table[:, tiles, NEG_SIN, :], in_=frac[:, SIN, :, :], func=ACT.Sin, scale=-2 * math.pi
+                out=table[:, tiles, COS, :], in_=size[:], func=ACT.Sin, scale=-2 * math.pi, bias=math.pi / 2
             )
 
         staged = {}
@@ -164,101 +170,120 @@ def tile_crossattnrope_pa_kernel(tc, x_in, coords, w_words, w_scales, out):
                 out=acc[:, first : first + width],
                 lhsT=codes[:, PASSES * s + g, :].bitcast(E5M2X4),
                 lhsT_scale=scales[:, PASSES * s + g, :],
-                rhs=w_codes[g][:, 2 * col : 2 * (col + width)].bitcast(E2M1X4),
+                rhs=w_codes[q][:, g, 2 * first : 2 * (first + width)].bitcast(E2M1X4),
                 rhs_scale=w_scale[:, g, col : col + width],
                 start=(g == 0),
                 stop=(g == PASSES - 1),
             )
 
-        def project(t):
-            accs = []
-            for q in range(BANKS_PER_TILE):
-                acc = acc_ps.tile([P, BANK_COLS], F32)
-                for group in GROUPS:
-                    for g in range(PASSES):
-                        mx_pass(acc, t, q, group, g)
-                accs.append(acc)
-            return accs
+        def project(t, q):
+            acc = acc_ps.tile([P, BANK_COLS], F32)
+            for group in GROUPS:
+                for g in range(PASSES):
+                    mx_pass(acc, t, q, group, g)
+            return acc
 
-        def multiply(terms, acc, t, q):
+        def multiply(terms, acc, t, heads):
             x12 = acc[:].rearrange("p (h a f i) -> p f h a i", a=AX, f=2, i=HALF)
-            heads = slice(HEADS_PER_BANK * q, HEADS_PER_BANK * (q + 1))
             for half, first in ((0, COS), (1, SIN)):
                 factors = table[:, t, first : first + 2, :].rearrange("p s (o a i) -> p s o a i", o=1, i=HALF)
                 nc.vector.tensor_tensor(
-                    out=terms[:, :, heads, :, half, :],
+                    out=terms[:, t % 2, :, heads, :, half, :],
                     in0=x12,
                     in1=factors.to_broadcast([P, 2, HEADS_PER_BANK, AX, HALF]),
                     op=ALU.mult,
                 )
 
-        def add_terms(engine, rotated, terms, heads):
-            flat = terms[:].rearrange("p c h a f i -> p c h (a f i)")
-            engine.tensor_tensor(out=rotated, in0=flat[:, 0, heads, :], in1=flat[:, 1, heads, :], op=ALU.add)
+        def add_terms(engine, rotated, terms, slots, heads):
+            flat = terms[:].rearrange("p s c h a f i -> p c h s (a f i)")
+            engine.tensor_tensor(
+                out=rotated, in0=flat[:, 0, heads, slots, :], in1=flat[:, 1, heads, slots, :], op=ALU.add
+            )
 
         def store(rotated, t, count, heads):
             b, j = divmod(t, TILES_PER_BATCH)
-            nc.sync.dma_start(out=out_rows[b][:, heads, DH * j : DH * (j + count)], in_=rotated)
+            nc.sync.dma_start(out=out_rows[b][:, heads, DH * j : DH * (j + count)], in_=rotated.rearrange("p h s d -> p h (s d)"))
 
         all_heads = slice(0, H)
 
-        def add_and_store(engine, terms, t, parts):
-            width = H // parts
-            for part in range(parts):
-                heads = slice(part * width, (part + 1) * width)
-                piece = work.tile([P, width, DH], F32, name="piece%d" % parts, bufs=max(parts, 2))
-                add_terms(engine, piece[:], terms, heads)
-                store(piece[:], t, 1, heads)
+        def add_and_store(engine, terms, t, count, heads):
+            n_heads = heads.stop - heads.start
+            piece = work.tile([P, n_heads, count, DH], F32, name="piece%d" % count, bufs=2 * count)
+            add_terms(engine, piece[:], terms, slice(t % 2, t % 2 + count), slice(0, n_heads))
+            store(piece[:], t, count, heads)
 
         def turn_pair(pair):
             open_pair(pair)
             for n in range(PASSES):
                 turn(pair, 2 * n, 2)
 
-        make_tables(slice(0, 2), drop_whole_turns(*count_turns(0, 2)))
-        later_turns = count_turns(2, n_t - 2)
+        def open_terms():
+            terms = work.tile([P, 2, 2, H, AX, 2, HALF], F32, bufs=2)
+            return terms
+
+        banks = range(BANKS_PER_TILE)
+        bank_heads = [slice(HEADS_PER_BANK * q, HEADS_PER_BANK * (q + 1)) for q in banks]
+        slot_a, slot_b = slice(0, 1), slice(1, 2)
+        gpsimd_heads, vector_heads = slice(0, H - SHARE), slice(H - SHARE, H)
+
+        frac = reduce_angles(0, 2)
+        make_sin(0, frac)
         open_pair(0)
-        turn(0, 0, 2)
-        turn(0, 2, 1)
+        for g in range(PASSES):
+            turn(0, g, 1)
+        make_cos_and_neg_sin(0, frac)
         quantize(0, 0, 2)
         quantize(0, 2, 1)
-        later_frac = drop_whole_turns(*later_turns)
+        turn(0, 3, 2)
+        turn(0, 5, 1)
+        later_frac = reduce_angles(2, n_t - 2)
+        quantize(0, 3, 2)
+        quantize(0, 5, 1)
 
-        for pair in range(PAIRS):
-            first, last = pair == 0, pair == PAIRS - 1
+        terms = rotated = None
+        for pair in range(PAIRS - 1):
+            first = pair == 0
             stored_together = pair < PAIRS - 2
             ta, tb = 2 * pair, 2 * pair + 1
-            if not first and not last:
+            if not first:
                 turn_pair(pair + 1)
-            accs = project(ta)
+            accs = [project(ta, q) for q in banks]
             if first:
-                turn(0, 3, 2)
-                turn(0, 5, 1)
                 turn_pair(1)
-                make_tables(slice(2, n_t), later_frac)
-            terms_a = work.tile([P, 2, H, AX, 2, HALF], F32, name="terms")
-            for q in range(BANKS_PER_TILE):
-                multiply(terms_a, accs[q], ta, q)
-                if first and q == 1:
-                    quantize(0, 3, 2)
-                    quantize(0, 5, 1)
-            if not last:
-                quantize(pair + 1, 0, 4)
+                make_sin(2, later_frac)
+                make_cos_and_neg_sin(2, later_frac)
+            terms_before, terms = terms, open_terms()
+            for q in banks:
+                multiply(terms, accs[q], ta, bank_heads[q])
+
+            quantize(pair + 1, 0, 4)
+            quantize(pair + 1, 4, 2)
+            if not first:
+                add_terms(nc.vector, rotated[:, vector_heads, slot_b, :], terms_before, slot_b, vector_heads)
+                store(rotated[:], ta - 2, 2, all_heads)
+
             if stored_together:
-                rotated = work.tile([P, H, 2 * DH], F32, name="rotated")
-                add_terms(nc.gpsimd, rotated[:, :, 0:DH], terms_a, all_heads)
+                rotated = work.tile([P, H, 2, DH], F32, bufs=2)
+                add_terms(nc.gpsimd, rotated[:, :, slot_a, :], terms, slot_a, all_heads)
             else:
-                add_and_store(nc.gpsimd, terms_a, ta, 2 if last else 1)
-            accs = project(tb)
-            terms_b = work.tile([P, 2, H, AX, 2, HALF], F32, name="terms")
-            for q in range(BANKS_PER_TILE):
-                multiply(terms_b, accs[q], tb, q)
-            if not last:
-                quantize(pair + 1, 4, 2)
+                add_and_store(nc.gpsimd, terms, ta, 1, all_heads)
+
+            accs = [project(tb, q) for q in banks]
+            for q in banks:
+                multiply(terms, accs[q], tb, bank_heads[q])
             if stored_together:
-                add_terms(nc.gpsimd, rotated[:, :, DH : 2 * DH], terms_b, all_heads)
-                store(rotated[:], ta, 2, all_heads)
-            elif not last:
-                add_and_store(nc.gpsimd, terms_b, tb, 1)
+                add_terms(nc.gpsimd, rotated[:, gpsimd_heads, slot_b, :], terms, slot_b, gpsimd_heads)
             else:
-                add_and_store(nc.vector, terms_b, tb, BANKS_PER_TILE)
+                add_and_store(nc.gpsimd, terms, tb, 1, all_heads)
+
+        ta = 2 * (PAIRS - 1)
+        bank_terms = []
+        for q in banks:
+            terms = work.tile([P, 2, 2, HEADS_PER_BANK, AX, 2, HALF], F32, name="bank_terms", bufs=BANKS_PER_TILE)
+            bank_terms.append(terms)
+            for t in (ta, ta + 1):
+                multiply(terms, project(t, q), t, bank_heads[0])
+            if q < BANKS_PER_TILE // 2:
+                add_and_store(nc.gpsimd, terms, ta, 2, bank_heads[q])
+        for q in banks[BANKS_PER_TILE // 2 :]:
+            add_and_store(nc.vector, bank_terms[q], ta, 2, bank_heads[q])

@@ -27,9 +27,8 @@ PAIRS = B * TILES_PER_BATCH // 2
 HEADS_PER_BANK = 4
 BANK_COLS = HEADS_PER_BANK * DH
 BANKS_PER_TILE = H // HEADS_PER_BANK
-SHARE = 4
+GROUP = 4
 GROUPS = ((0, 256), (256, 128))
-SIN, COS, NEG_SIN = 0, 1, 2
 
 
 def tile_crossattnrope_pa_kernel(tc, x_in, coords, w_words, w_scales, out):
@@ -63,25 +62,27 @@ def tile_crossattnrope_pa_kernel(tc, x_in, coords, w_words, w_scales, out):
 
         w_codes = []
 
-        def load_w(q):
-            wc = keep.tile([P, PASSES, 2 * BANK_COLS], U8, name="w_codes%d" % q, align_bytes=64)
-            cols = slice(2 * BANK_COLS * q, 2 * BANK_COLS * (q + 1))
+        def load_w(q0, count):
+            width = 2 * BANK_COLS
+            wc = keep.tile([P, PASSES, width * count], U8, name="w_codes%d" % q0, align_bytes=64)
+            cols = slice(width * q0, width * (q0 + count))
             nc.sync.dma_start(
                 out=wc[:].bitcast(I32), in_=w_words[:, :, cols].rearrange("g p n -> p g n").bitcast(I32)
             )
-            w_codes.append(wc)
+            w_codes.extend(wc[:, :, width * n : width * (n + 1)] for n in range(count))
 
         load_x(0, 1)
         load_x(1, 1)
-        load_w(0)
+        load_w(0, 1)
         for q in range(4):
             nc.sync.dma_start(
                 out=w_scale[32 * q : 32 * q + 4, :, :].bitcast(I32),
                 in_=w_scales[:, 4 * q : 4 * q + 4, :].rearrange("g r n -> r g n").bitcast(I32),
             )
-        for q in range(1, BANKS_PER_TILE):
-            load_w(q)
-        for pair in range(1, PAIRS):
+        load_x(2, 1)
+        load_x(3, 1)
+        load_w(1, BANKS_PER_TILE - 1)
+        for pair in range(2, PAIRS):
             load_x(2 * pair, 2)
 
         ones = keep.tile([P, 1], F32)
@@ -99,9 +100,9 @@ def tile_crossattnrope_pa_kernel(tc, x_in, coords, w_words, w_scales, out):
         n_t = B * TILES_PER_BATCH
         per_tile = AX * HALF
         coord_cols = coord_sb[:].rearrange("p b c -> p (b c)")
-        table = keep.tile([P, n_t, 3, per_tile], F32)
+        table = keep.tile([P, 2, n_t, AX, 2, HALF], F32)
 
-        def reduce_angles(t0, count):
+        def count_turns(t0, count):
             turns = keep.tile([P, count * per_tile], F32, name="turns%d" % t0)
             shape = [P, count * AX, HALF]
             nc.vector.tensor_tensor(
@@ -112,31 +113,39 @@ def tile_crossattnrope_pa_kernel(tc, x_in, coords, w_words, w_scales, out):
             )
             whole = keep.tile([P, count * per_tile], I32, name="whole%d" % t0)
             nc.vector.tensor_copy(out=whole[:], in_=turns[:])
-            frac = keep.tile([P, count, per_tile], F32, name="frac%d" % t0)
+            return turns, whole
+
+        def drop_whole_turns(t0, count, turns, whole):
+            frac = keep.tile([P, count, AX, HALF], F32, name="frac%d" % t0)
             nc.vector.tensor_tensor(
-                out=frac[:].rearrange("p t x -> p (t x)"), in0=turns[:], in1=whole[:], op=ALU.subtract
+                out=frac[:].rearrange("p t a i -> p (t a i)"), in0=turns[:], in1=whole[:], op=ALU.subtract
             )
             return frac
 
         def make_sin(t0, frac):
             tiles = slice(t0, t0 + frac.shape[1])
-            nc.scalar.activation(out=table[:, tiles, SIN, :], in_=frac[:], func=ACT.Sin, scale=2 * math.pi)
+            nc.scalar.activation(out=table[:, 1, tiles, :, 0, :], in_=frac[:], func=ACT.Sin, scale=2 * math.pi)
 
         def make_cos_and_neg_sin(t0, frac):
             tiles = slice(t0, t0 + frac.shape[1])
             size = keep.tile(frac.shape, F32, name="size%d" % t0)
             nc.scalar.activation(out=size[:], in_=frac[:], func=ACT.Abs)
-            nc.scalar.activation(out=table[:, tiles, NEG_SIN, :], in_=frac[:], func=ACT.Sin, scale=-2 * math.pi)
-            nc.scalar.activation(
-                out=table[:, tiles, COS, :], in_=size[:], func=ACT.Sin, scale=-2 * math.pi, bias=math.pi / 2
-            )
+            nc.scalar.activation(out=table[:, 0, tiles, :, 1, :], in_=frac[:], func=ACT.Sin, scale=-2 * math.pi)
+            for half in range(2):
+                nc.scalar.activation(
+                    out=table[:, half, tiles, :, half, :],
+                    in_=size[:],
+                    func=ACT.Sin,
+                    scale=-2 * math.pi,
+                    bias=math.pi / 2,
+                )
 
         staged = {}
 
         def open_pair(pair):
             grouped = work.tile([P, 2 * PASSES, 512], BF16, align_bytes=64)
-            codes = work.tile([P, 2 * PASSES, P], U32, align_bytes=64)
-            scales = work.tile([P, 2 * PASSES, P], U8, align_bytes=64)
+            codes = work.tile([P, 2 * PASSES, P], U32, align_bytes=64, bufs=4)
+            scales = work.tile([P, 2 * PASSES, P], U8, align_bytes=64, bufs=4)
             staged[pair] = (grouped, codes, scales)
 
         def turn(pair, first, count):
@@ -183,107 +192,102 @@ def tile_crossattnrope_pa_kernel(tc, x_in, coords, w_words, w_scales, out):
                     mx_pass(acc, t, q, group, g)
             return acc
 
-        def multiply(terms, acc, t, heads):
-            x12 = acc[:].rearrange("p (h a f i) -> p f h a i", a=AX, f=2, i=HALF)
-            for half, first in ((0, COS), (1, SIN)):
-                factors = table[:, t, first : first + 2, :].rearrange("p s (o a i) -> p s o a i", o=1, i=HALF)
-                nc.vector.tensor_tensor(
-                    out=terms[:, t % 2, :, heads, :, half, :],
-                    in0=x12,
-                    in1=factors.to_broadcast([P, 2, HEADS_PER_BANK, AX, HALF]),
-                    op=ALU.mult,
-                )
-
-        def add_terms(engine, rotated, terms, slots, heads):
-            flat = terms[:].rearrange("p s c h a f i -> p c h s (a f i)")
-            engine.tensor_tensor(
-                out=rotated, in0=flat[:, 0, heads, slots, :], in1=flat[:, 1, heads, slots, :], op=ALU.add
+        def multiply(terms, acc, t):
+            shape = [P, 2, HEADS_PER_BANK, DH]
+            nc.vector.tensor_tensor(
+                out=terms[:, :, :, t % GROUP, :],
+                in0=acc[:].rearrange("p (o h d) -> p o h d", o=1, d=DH).to_broadcast(shape),
+                in1=table[:, :, t : t + 1, :, :, :].rearrange("p o t a f i -> p o t (a f i)").to_broadcast(shape),
+                op=ALU.mult,
             )
 
-        def store(rotated, t, count, heads):
-            b, j = divmod(t, TILES_PER_BATCH)
-            nc.sync.dma_start(out=out_rows[b][:, heads, DH * j : DH * (j + count)], in_=rotated.rearrange("p h s d -> p h (s d)"))
+        def open_unit():
+            terms = work.tile([P, 2, HEADS_PER_BANK, GROUP, DH], F32, bufs=3)
+            rotated = work.tile([P, HEADS_PER_BANK, GROUP, DH], F32, bufs=4)
+            return terms, rotated
 
-        all_heads = slice(0, H)
+        def add_terms(engine, unit, first, count):
+            terms, rotated = unit
+            heads = slice(first, first + count)
+            by_block = terms[:, :, heads, :, :].rearrange("p o h s (a f i) -> p f (h s a) o i", f=2, i=HALF)
+            engine.tensor_tensor(
+                out=rotated[:, heads, :, :].rearrange("p h s (a o i) -> p (h s a) o i", o=2, i=HALF),
+                in0=by_block[:, 0, :, :, :],
+                in1=by_block[:, 1, :, :, :],
+                op=ALU.add,
+            )
 
-        def add_and_store(engine, terms, t, count, heads):
-            n_heads = heads.stop - heads.start
-            piece = work.tile([P, n_heads, count, DH], F32, name="piece%d" % count, bufs=2 * count)
-            add_terms(engine, piece[:], terms, slice(t % 2, t % 2 + count), slice(0, n_heads))
-            store(piece[:], t, count, heads)
+        def store(unit, group, q, first, count):
+            b, j = divmod(GROUP * group, TILES_PER_BATCH)
+            head = HEADS_PER_BANK * q + first
+            nc.sync.dma_start(
+                out=out_rows[b][:, head : head + count, DH * j : DH * (j + GROUP)],
+                in_=unit[1][:, first : first + count, :, :].rearrange("p h s d -> p h (s d)"),
+            )
 
         def turn_pair(pair):
             open_pair(pair)
             for n in range(PASSES):
                 turn(pair, 2 * n, 2)
 
-        def open_terms():
-            terms = work.tile([P, 2, 2, H, AX, 2, HALF], F32, bufs=2)
-            return terms
+        def turn_tile(t):
+            turn(t // 2, PASSES * (t % 2), 2)
+            turn(t // 2, PASSES * (t % 2) + 2, 1)
 
-        banks = range(BANKS_PER_TILE)
-        bank_heads = [slice(HEADS_PER_BANK * q, HEADS_PER_BANK * (q + 1)) for q in banks]
-        slot_a, slot_b = slice(0, 1), slice(1, 2)
-        gpsimd_heads, vector_heads = slice(0, H - SHARE), slice(H - SHARE, H)
+        def quantize_tile(t):
+            quantize(t // 2, PASSES * (t % 2), 2)
+            quantize(t // 2, PASSES * (t % 2) + 2, 1)
 
-        frac = reduce_angles(0, 2)
+        frac = drop_whole_turns(0, GROUP, *count_turns(0, GROUP))
         make_sin(0, frac)
         open_pair(0)
+        open_pair(1)
         for g in range(PASSES):
             turn(0, g, 1)
         make_cos_and_neg_sin(0, frac)
-        quantize(0, 0, 2)
-        quantize(0, 2, 1)
-        turn(0, 3, 2)
-        turn(0, 5, 1)
-        later_frac = reduce_angles(2, n_t - 2)
-        quantize(0, 3, 2)
-        quantize(0, 5, 1)
+        quantize_tile(0)
+        turn_tile(1)
+        later_turns = count_turns(GROUP, n_t - GROUP)
+        quantize_tile(1)
+        unit = open_unit()
+        for t in range(GROUP):
+            acc = project(t, 0)
+            if t + 2 < GROUP:
+                turn_tile(t + 2)
+            multiply(unit[0], acc, t)
+            if t == 0:
+                later_frac = drop_whole_turns(GROUP, n_t - GROUP, *later_turns)
+            if t + 2 < GROUP:
+                quantize_tile(t + 2)
+        make_sin(GROUP, later_frac)
+        make_cos_and_neg_sin(GROUP, later_frac)
+        add_terms(nc.gpsimd, unit, 0, HEADS_PER_BANK)
+        store(unit, 0, 0, 0, HEADS_PER_BANK)
 
-        terms = rotated = None
-        for pair in range(PAIRS - 1):
-            first = pair == 0
-            stored_together = pair < PAIRS - 2
-            ta, tb = 2 * pair, 2 * pair + 1
-            if not first:
-                turn_pair(pair + 1)
-            accs = [project(ta, q) for q in banks]
-            if first:
-                turn_pair(1)
-                make_sin(2, later_frac)
-                make_cos_and_neg_sin(2, later_frac)
-            terms_before, terms = terms, open_terms()
-            for q in banks:
-                multiply(terms, accs[q], ta, bank_heads[q])
-
-            quantize(pair + 1, 0, 4)
-            quantize(pair + 1, 4, 2)
-            if not first:
-                add_terms(nc.vector, rotated[:, vector_heads, slot_b, :], terms_before, slot_b, vector_heads)
-                store(rotated[:], ta - 2, 2, all_heads)
-
-            if stored_together:
-                rotated = work.tile([P, H, 2, DH], F32, bufs=2)
-                add_terms(nc.gpsimd, rotated[:, :, slot_a, :], terms, slot_a, all_heads)
-            else:
-                add_and_store(nc.gpsimd, terms, ta, 1, all_heads)
-
-            accs = [project(tb, q) for q in banks]
-            for q in banks:
-                multiply(terms, accs[q], tb, bank_heads[q])
-            if stored_together:
-                add_terms(nc.gpsimd, rotated[:, gpsimd_heads, slot_b, :], terms, slot_b, gpsimd_heads)
-            else:
-                add_and_store(nc.gpsimd, terms, tb, 1, all_heads)
-
-        ta = 2 * (PAIRS - 1)
-        bank_terms = []
-        for q in banks:
-            terms = work.tile([P, 2, 2, HEADS_PER_BANK, AX, 2, HALF], F32, name="bank_terms", bufs=BANKS_PER_TILE)
-            bank_terms.append(terms)
-            for t in (ta, ta + 1):
-                multiply(terms, project(t, q), t, bank_heads[0])
-            if q < BANKS_PER_TILE // 2:
-                add_and_store(nc.gpsimd, terms, ta, 2, bank_heads[q])
-        for q in banks[BANKS_PER_TILE // 2 :]:
-            add_and_store(nc.vector, bank_terms[q], ta, 2, bank_heads[q])
+        groups = n_t // GROUP
+        for group in range(groups):
+            more = group + 1 < groups
+            for q in range(1 if group == 0 else 0, BANKS_PER_TILE):
+                tiles = range(GROUP * group, GROUP * (group + 1))
+                accs = [project(t, q) for t in tiles]
+                next_pair = 2 * (group + 1) + q - 2
+                hand_over = more and q >= 2
+                if hand_over:
+                    turn_pair(next_pair)
+                unit = open_unit()
+                for t in tiles:
+                    multiply(unit[0], accs[t % GROUP], t)
+                if hand_over:
+                    quantize(next_pair, 0, 4)
+                    quantize(next_pair, 4, 2)
+                if more or q < 2:
+                    add_terms(nc.gpsimd, unit, 0, HEADS_PER_BANK)
+                    store(unit, group, q, 0, HEADS_PER_BANK)
+                elif q == 2:
+                    for first in (0, 2):
+                        add_terms(nc.gpsimd, unit, first, 2)
+                        store(unit, group, q, first, 2)
+                else:
+                    for first in range(HEADS_PER_BANK):
+                        add_terms(nc.vector, unit, first, 1)
+                        store(unit, group, q, first, 1)

import math
from contextlib import ExitStack

import concourse.mybir as mybir
from concourse.masks import make_identity

B, L, C, H, DH, AX = 2, 1024, 1536, 16, 96, 3
HALF = 16
BLK = 2 * HALF
ROPE_BASE = 10000.0
FLOPS = 2 * B * L * C * H * DH

F32 = mybir.dt.float32
BF16 = mybir.dt.bfloat16
I32 = mybir.dt.int32
U32 = mybir.dt.uint32
U8 = mybir.dt.uint8
E5M2X4 = mybir.dt.float8_e5m2_x4
E2M1X4 = mybir.dt.float4_e2m1fn_x4
ALU = mybir.AluOpType
ACT = mybir.ActivationFunctionType

P = 128
PASSES = C // 512
TILES_PER_BATCH = L // P
PAIRS = B * TILES_PER_BATCH // 2
HEADS_PER_BANK = 4
BANK_COLS = HEADS_PER_BANK * DH
BANKS_PER_TILE = H // HEADS_PER_BANK
GROUP = 4
GROUPS = ((0, 256), (256, 128))


def tile_crossattnrope_pa_kernel(tc, x_in, coords, w_words, w_scales, out):
    nc = tc.nc
    x_rows = [x_in[b].rearrange("(p j) k -> p j k", j=TILES_PER_BATCH) for b in range(B)]
    out_rows = [out[b].rearrange("h (p j) d -> p h (j d)", j=TILES_PER_BATCH) for b in range(B)]

    with ExitStack() as ctx:
        keep = ctx.enter_context(tc.tile_pool(name="keep", bufs=1))
        work = ctx.enter_context(tc.tile_pool(name="work", bufs=2))
        turn_ps = ctx.enter_context(tc.psum_pool(name="turn_ps", bufs=3))
        acc_ps = ctx.enter_context(tc.psum_pool(name="acc_ps", bufs=5))
        ctx.enter_context(tc.manual_schedule())

        w_scale = keep.tile([P, PASSES, C], U8, align_bytes=64)
        nc.vector.memset(w_scale[:].bitcast(I32), 0)
        ident = keep.tile([P, P], F32)
        make_identity(nc, ident[:])

        coord_sb = keep.tile([P, B, TILES_PER_BATCH * AX], BF16)
        nc.sync.dma_start(out=coord_sb[:], in_=coords.rearrange("b (p j) a -> p b (j a)", j=TILES_PER_BATCH))

        x_sb = {}

        def load_x(t0, count):
            b, j = divmod(t0, TILES_PER_BATCH)
            xt = keep.tile([P, count, C], BF16, name="x%d" % t0, align_bytes=64)
            nc.sync.dma_start(out=xt[:], in_=x_rows[b][:, j : j + count, :])
            for s in range(count):
                x_sb[t0 + s] = xt[:, s, :]

        w_codes = []

        def load_w(q0, count):
            width = 2 * BANK_COLS
            wc = keep.tile([P, PASSES, width * count], U8, name="w_codes%d" % q0, align_bytes=64)
            cols = slice(width * q0, width * (q0 + count))
            nc.sync.dma_start(
                out=wc[:].bitcast(I32), in_=w_words[:, :, cols].rearrange("g p n -> p g n").bitcast(I32)
            )
            w_codes.extend(wc[:, :, width * n : width * (n + 1)] for n in range(count))

        load_x(0, 1)
        load_x(1, 1)
        load_w(0, 1)
        for q in range(4):
            nc.sync.dma_start(
                out=w_scale[32 * q : 32 * q + 4, :, :].bitcast(I32),
                in_=w_scales[:, 4 * q : 4 * q + 4, :].rearrange("g r n -> r g n").bitcast(I32),
            )
        load_x(2, 1)
        load_x(3, 1)
        load_w(1, BANKS_PER_TILE - 1)
        for pair in range(2, PAIRS):
            load_x(2 * pair, 2)

        ones = keep.tile([P, 1], F32)
        nc.vector.memset(ones[:], 1.0)
        turns_per_unit = keep.tile([P, 1, HALF], F32)
        for i in range(HALF):
            nc.vector.tensor_scalar(
                out=turns_per_unit[:, 0, i : i + 1],
                in0=ones[:],
                scalar1=ROPE_BASE ** (-i / HALF) / (2 * math.pi),
                scalar2=None,
                op0=ALU.mult,
            )

        n_t = B * TILES_PER_BATCH
        per_tile = AX * HALF
        coord_cols = coord_sb[:].rearrange("p b c -> p (b c)")
        table = keep.tile([P, 2, n_t, AX, 2, HALF], F32)

        def count_turns(t0, count):
            turns = keep.tile([P, count * per_tile], F32, name="turns%d" % t0)
            shape = [P, count * AX, HALF]
            nc.vector.tensor_tensor(
                out=turns[:].rearrange("p (c i) -> p c i", i=HALF),
                in0=coord_cols[:, AX * t0 : AX * (t0 + count)].unsqueeze(2).to_broadcast(shape),
                in1=turns_per_unit[:].to_broadcast(shape),
                op=ALU.mult,
            )
            whole = keep.tile([P, count * per_tile], I32, name="whole%d" % t0)
            nc.vector.tensor_copy(out=whole[:], in_=turns[:])
            return turns, whole

        def drop_whole_turns(t0, count, turns, whole):
            frac = keep.tile([P, count, AX, HALF], F32, name="frac%d" % t0)
            nc.vector.tensor_tensor(
                out=frac[:].rearrange("p t a i -> p (t a i)"), in0=turns[:], in1=whole[:], op=ALU.subtract
            )
            return frac

        def make_sin(t0, frac):
            tiles = slice(t0, t0 + frac.shape[1])
            nc.scalar.activation(out=table[:, 1, tiles, :, 0, :], in_=frac[:], func=ACT.Sin, scale=2 * math.pi)

        def make_cos_and_neg_sin(t0, frac):
            tiles = slice(t0, t0 + frac.shape[1])
            size = keep.tile(frac.shape, F32, name="size%d" % t0)
            nc.scalar.activation(out=size[:], in_=frac[:], func=ACT.Abs)
            nc.scalar.activation(out=table[:, 0, tiles, :, 1, :], in_=frac[:], func=ACT.Sin, scale=-2 * math.pi)
            for half in range(2):
                nc.scalar.activation(
                    out=table[:, half, tiles, :, half, :],
                    in_=size[:],
                    func=ACT.Sin,
                    scale=-2 * math.pi,
                    bias=math.pi / 2,
                )

        staged = {}

        def open_pair(pair):
            grouped = work.tile([P, 2 * PASSES, 512], BF16, align_bytes=64)
            codes = work.tile([P, 2 * PASSES, P], U32, align_bytes=64, bufs=4)
            scales = work.tile([P, 2 * PASSES, P], U8, align_bytes=64, bufs=4)
            staged[pair] = (grouped, codes, scales)

        def turn(pair, first, count):
            grouped = staged[pair][0]
            bank = turn_ps.tile([P, 2, 2, P], F32)
            for n in range(count):
                s, g = divmod(first + n, PASSES)
                words = x_sb[2 * pair + s].bitcast(F32)
                for u in range(2):
                    nc.tensor.transpose(bank[:, n, u, :], words[:, 256 * g + u : 256 * (g + 1) : 2], ident[:])
            nc.scalar.copy(
                out=grouped[:, first : first + count, :].bitcast(F32).rearrange("p n (r u) -> p n r u", u=2),
                in_=bank[:, 0:count, :, :].rearrange("p n u r -> p n r u"),
            )

        def quantize(pair, first, count):
            grouped, codes, scales = staged[pair]
            units = slice(first, first + count)
            nc.vector.quantize_mx(
                out=codes[:, units, :].rearrange("p n r -> p (n r)").bitcast(E5M2X4),
                scales=scales[:, units, :].rearrange("p n r -> p (n r)"),
                in_=grouped[:, units, :].rearrange("p n c -> p (n c)"),
            )

        def mx_pass(acc, t, q, group, g):
            pair, s = divmod(t, 2)
            codes, scales = staged[pair][1:]
            first, width = group
            col = BANK_COLS * q + first
            nc.tensor.matmul_mx(
                out=acc[:, first : first + width],
                lhsT=codes[:, PASSES * s + g, :].bitcast(E5M2X4),
                lhsT_scale=scales[:, PASSES * s + g, :],
                rhs=w_codes[q][:, g, 2 * first : 2 * (first + width)].bitcast(E2M1X4),
                rhs_scale=w_scale[:, g, col : col + width],
                start=(g == 0),
                stop=(g == PASSES - 1),
            )

        def project(t, q):
            acc = acc_ps.tile([P, BANK_COLS], F32)
            for group in GROUPS:
                for g in range(PASSES):
                    mx_pass(acc, t, q, group, g)
            return acc

        def multiply(terms, acc, t):
            shape = [P, 2, HEADS_PER_BANK, DH]
            nc.vector.tensor_tensor(
                out=terms[:, :, :, t % GROUP, :],
                in0=acc[:].rearrange("p (o h d) -> p o h d", o=1, d=DH).to_broadcast(shape),
                in1=table[:, :, t : t + 1, :, :, :].rearrange("p o t a f i -> p o t (a f i)").to_broadcast(shape),
                op=ALU.mult,
            )

        def open_unit():
            terms = work.tile([P, 2, HEADS_PER_BANK, GROUP, DH], F32, bufs=3)
            rotated = work.tile([P, HEADS_PER_BANK, GROUP, DH], F32, bufs=4)
            return terms, rotated

        def add_terms(engine, unit, first, count):
            terms, rotated = unit
            heads = slice(first, first + count)
            by_block = terms[:, :, heads, :, :].rearrange("p o h s (a f i) -> p f (h s a) o i", f=2, i=HALF)
            engine.tensor_tensor(
                out=rotated[:, heads, :, :].rearrange("p h s (a o i) -> p (h s a) o i", o=2, i=HALF),
                in0=by_block[:, 0, :, :, :],
                in1=by_block[:, 1, :, :, :],
                op=ALU.add,
            )

        def store(unit, group, q, first, count):
            b, j = divmod(GROUP * group, TILES_PER_BATCH)
            head = HEADS_PER_BANK * q + first
            nc.sync.dma_start(
                out=out_rows[b][:, head : head + count, DH * j : DH * (j + GROUP)],
                in_=unit[1][:, first : first + count, :, :].rearrange("p h s d -> p h (s d)"),
            )

        def turn_pair(pair):
            open_pair(pair)
            for n in range(PASSES):
                turn(pair, 2 * n, 2)

        def turn_tile(t):
            turn(t // 2, PASSES * (t % 2), 2)
            turn(t // 2, PASSES * (t % 2) + 2, 1)

        def quantize_tile(t):
            quantize(t // 2, PASSES * (t % 2), 2)
            quantize(t // 2, PASSES * (t % 2) + 2, 1)

        frac = drop_whole_turns(0, GROUP, *count_turns(0, GROUP))
        make_sin(0, frac)
        open_pair(0)
        open_pair(1)
        for g in range(PASSES):
            turn(0, g, 1)
        make_cos_and_neg_sin(0, frac)
        quantize_tile(0)
        turn_tile(1)
        later_turns = count_turns(GROUP, n_t - GROUP)
        quantize_tile(1)
        unit = open_unit()
        for t in range(GROUP):
            acc = project(t, 0)
            if t + 2 < GROUP:
                turn_tile(t + 2)
            multiply(unit[0], acc, t)
            if t == 0:
                later_frac = drop_whole_turns(GROUP, n_t - GROUP, *later_turns)
            if t + 2 < GROUP:
                quantize_tile(t + 2)
        make_sin(GROUP, later_frac)
        make_cos_and_neg_sin(GROUP, later_frac)
        add_terms(nc.gpsimd, unit, 0, HEADS_PER_BANK)
        store(unit, 0, 0, 0, HEADS_PER_BANK)

        groups = n_t // GROUP
        for group in range(groups):
            more = group + 1 < groups
            for q in range(1 if group == 0 else 0, BANKS_PER_TILE):
                tiles = range(GROUP * group, GROUP * (group + 1))
                accs = [project(t, q) for t in tiles]
                next_pair = 2 * (group + 1) + q - 2
                hand_over = more and q >= 2
                if hand_over:
                    turn_pair(next_pair)
                unit = open_unit()
                for t in tiles:
                    multiply(unit[0], accs[t % GROUP], t)
                if hand_over:
                    quantize(next_pair, 0, 4)
                    quantize(next_pair, 4, 2)
                if more or q < 2:
                    add_terms(nc.gpsimd, unit, 0, HEADS_PER_BANK)
                    store(unit, group, q, 0, HEADS_PER_BANK)
                elif q == 2:
                    for first in (0, 2):
                        add_terms(nc.gpsimd, unit, first, 2)
                        store(unit, group, q, first, 2)
                else:
                    for first in range(HEADS_PER_BANK):
                        add_terms(nc.vector, unit, first, 1)
                        store(unit, group, q, first, 1)
